import numpy as np
import ml_dtypes

BF16 = ml_dtypes.bfloat16


def bf(x):
    return np.asarray(x, np.float32).astype(BF16)


def f32(x):
    return np.asarray(x, np.float32)


def f64(x):
    return np.asarray(x).astype(np.float64)


def striped(idx):
    return np.tile(idx.reshape(-1, 16).T, (8, 1))


C, D, S, N, H, H2, HID, HALF = 256, 256, 4096, 1024, 16, 8, 16, 128
W_COL, W_ROW, B_COL, B_ROW, LO, HI = 0.4, -0.3, 3.0, 0.2, 0.9, 1.0


def per_head(v):
    return f32(np.repeat(v, HID)[:, None])


def setup_inputs():
    col = np.arange(H) < H2
    w_mix = np.where(col, W_COL, W_ROW) * (1.0 + 0.1 * np.random.standard_normal(H))
    b_mix = np.where(col, B_COL, B_ROW) * (1.0 + 0.1 * np.random.standard_normal(H))
    decay = 0.75 + 0.35 * np.random.random(H)
    return {"base": f32(np.random.standard_normal((C, S))), "x": bf(np.random.standard_normal((D, N))), "w_proj": bf(np.random.standard_normal((D, C)) / np.sqrt(D)), "b_proj": f32(0.3 * np.random.standard_normal((C, 1))), "w_mix": per_head(w_mix), "b_mix": per_head(b_mix), "decay": per_head(decay), "cache": f32(np.random.standard_normal((C, N))), "offs": striped(np.random.permutation(S)[:N])}


def reference(base, x, w_proj, b_proj, w_mix, b_mix, decay, cache, offs):
    idx = offs[:16].T.reshape(-1)
    proj = f64(w_proj).T @ f64(x) + f64(b_proj)
    dec = np.minimum(np.maximum(f64(decay), LO), HI)
    coef = np.where(np.arange(C)[:, None] < HALF, f64(w_mix) * dec, dec)
    out = f64(base).copy()
    out[:, idx] = (f64(w_mix) * proj + f64(b_mix)) + coef * f64(cache)
    return out

@@ -1,0 +1,100 @@
+import concourse.mybir as mybir
+from concourse.masks import make_identity
+
+P = 128
+C, D, S, N = 256, 256, 4096, 1024
+HALF = 128
+LO, HI = 0.9, 1.0
+BANK = 512
+C_BLOCKS, D_BLOCKS, N_BANKS = C // P, D // P, N // BANK
+
+FLOPS = 2 * C * D * N
+
+F32, BF16, U16 = mybir.dt.float32, mybir.dt.bfloat16, mybir.dt.uint16
+ADD, MULT, MAX, MIN = (
+    mybir.AluOpType.add,
+    mybir.AluOpType.mult,
+    mybir.AluOpType.max,
+    mybir.AluOpType.min,
+)
+IDENTITY = mybir.ActivationFunctionType.Identity
+
+
+def tile_mixedrepeatheads_kernel(
+    tc, base, x, w_proj, b_proj, w_mix, b_mix, decay, cache, offs, out
+):
+    nc = tc.nc
+    with (
+        tc.tile_pool(name="held", bufs=1) as held,
+        tc.psum_pool(name="psum", bufs=1) as psum,
+    ):
+        offsets = held.tile([P, N // 16], U16, name="offsets")
+        nc.sync.dma_start(offsets[:], offs)
+
+        vectors = (b_proj, w_mix, b_mix, decay)
+        rows = held.tile([P, P], F32, name="rows")
+        nc.vector.memset(rows[:], 0.0)
+        for v, vector in enumerate(vectors):
+            nc.scalar.dma_start(
+                rows[v * C_BLOCKS : (v + 1) * C_BLOCKS, :],
+                vector.rearrange("(b p) o -> b (p o)", p=P),
+            )
+
+        weights = held.tile([P, D_BLOCKS, C], BF16, name="weights")
+        nc.sync.dma_start(weights[:], w_proj.rearrange("(k p) c -> p k c", p=P))
+        features = held.tile([P, D_BLOCKS, N], BF16, name="features")
+        nc.sync.dma_start(features[:], x.rearrange("(k p) n -> p k n", p=P))
+        cached, windows = [], []
+        for b in range(C_BLOCKS):
+            channels = slice(b * P, (b + 1) * P)
+            cached.append(held.tile([P, N], F32, name=f"cached{b}"))
+            nc.sync.dma_start(cached[b][:], cache[channels, :])
+            windows.append(held.tile([P, S], F32, name=f"window{b}"))
+            nc.sync.dma_start(windows[b][:], base[channels, :])
+
+        identity = held.tile([P, P], F32, name="identity")
+        make_identity(nc, identity[:])
+        columns_psum = psum.tile([P, P], F32, name="columns_psum")
+        nc.tensor.transpose(columns_psum[:], rows[:], identity[:])
+        columns = held.tile([P, len(vectors) * C_BLOCKS], F32, name="columns")
+        nc.vector.tensor_copy(columns[:], columns_psum[:, 0 : len(vectors) * C_BLOCKS])
+        b_proj_col, w_mix_col, b_mix_col, decay_col = (
+            columns[:, v * C_BLOCKS : (v + 1) * C_BLOCKS] for v in range(len(vectors))
+        )
+
+        coef = held.tile([P, C_BLOCKS], F32, name="coef")
+        nc.vector.tensor_scalar(coef[:], decay_col, LO, HI, MAX, MIN)
+        column_heads = slice(0, HALF // P)
+        nc.vector.tensor_tensor(
+            coef[:, column_heads], coef[:, column_heads], w_mix_col[:, column_heads], MULT
+        )
+        shift = held.tile([P, C_BLOCKS], F32, name="shift")
+        nc.vector.tensor_tensor(shift[:], w_mix_col, b_proj_col, MULT)
+        nc.vector.tensor_tensor(shift[:], shift[:], b_mix_col, ADD)
+
+        for b in range(C_BLOCKS):
+            channels = slice(b * P, (b + 1) * P)
+            mixed = held.tile([P, N], F32, name=f"mixed{b}")
+            for h in range(N_BANKS):
+                entries = slice(h * BANK, (h + 1) * BANK)
+                proj = psum.tile([P, BANK], F32, name=f"proj{b}_{h}")
+                for k in range(D_BLOCKS):
+                    nc.tensor.matmul(
+                        proj[:],
+                        weights[:, k, channels],
+                        features[:, k, entries],
+                        start=(k == 0),
+                        stop=(k == D_BLOCKS - 1),
+                    )
+                nc.scalar.activation(
+                    mixed[:, entries],
+                    proj[:],
+                    IDENTITY,
+                    bias=shift[:, b : b + 1],
+                    scale=w_mix_col[:, b : b + 1],
+                )
+            decayed = held.tile([P, N], F32, name=f"decayed{b}")
+            nc.scalar.activation(decayed[:], cached[b][:], IDENTITY, scale=coef[:, b : b + 1])
+
+            nc.vector.tensor_tensor(windows[b][:].indirect(offsets[:]), mixed[:], decayed[:], ADD)
+            nc.sync.dma_start(out[channels, :], windows[b][:])

@@ -1,5 +1,4 @@
 import concourse.mybir as mybir
-from concourse.masks import make_identity
 
 P = 128
 C, D, S, N = 256, 256, 4096, 1024
@@ -31,14 +30,17 @@ def tile_mixedrepeatheads_kernel(
         offsets = held.tile([P, N // 16], U16, name="offsets")
         nc.sync.dma_start(offsets[:], offs)
 
-        vectors = (b_proj, w_mix, b_mix, decay)
-        rows = held.tile([P, P], F32, name="rows")
-        nc.vector.memset(rows[:], 0.0)
-        for v, vector in enumerate(vectors):
-            nc.scalar.dma_start(
-                rows[v * C_BLOCKS : (v + 1) * C_BLOCKS, :],
-                vector.rearrange("(b p) o -> b (p o)", p=P),
-            )
+        b_proj_col, w_mix_col, b_mix_col, decay_col = (
+            held.tile([P, C_BLOCKS], F32, name=name)
+            for name in ("b_proj_col", "w_mix_col", "b_mix_col", "decay_col")
+        )
+        for column, vector in (
+            (w_mix_col, w_mix),
+            (b_proj_col, b_proj),
+            (b_mix_col, b_mix),
+            (decay_col, decay),
+        ):
+            nc.scalar.dma_start(column[:], vector.rearrange("(b p) o -> p (b o)", p=P))
 
         weights = held.tile([P, D_BLOCKS, C], BF16, name="weights")
         nc.sync.dma_start(weights[:], w_proj.rearrange("(k p) c -> p k c", p=P))
@@ -52,25 +54,15 @@ def tile_mixedrepeatheads_kernel(
             windows.append(held.tile([P, S], F32, name=f"window{b}"))
             nc.sync.dma_start(windows[b][:], base[channels, :])
 
-        identity = held.tile([P, P], F32, name="identity")
-        make_identity(nc, identity[:])
-        columns_psum = psum.tile([P, P], F32, name="columns_psum")
-        nc.tensor.transpose(columns_psum[:], rows[:], identity[:])
-        columns = held.tile([P, len(vectors) * C_BLOCKS], F32, name="columns")
-        nc.vector.tensor_copy(columns[:], columns_psum[:, 0 : len(vectors) * C_BLOCKS])
-        b_proj_col, w_mix_col, b_mix_col, decay_col = (
-            columns[:, v * C_BLOCKS : (v + 1) * C_BLOCKS] for v in range(len(vectors))
-        )
-
         coef = held.tile([P, C_BLOCKS], F32, name="coef")
-        nc.vector.tensor_scalar(coef[:], decay_col, LO, HI, MAX, MIN)
+        nc.vector.tensor_scalar(coef[:], decay_col[:], LO, HI, MAX, MIN)
         column_heads = slice(0, HALF // P)
         nc.vector.tensor_tensor(
             coef[:, column_heads], coef[:, column_heads], w_mix_col[:, column_heads], MULT
         )
         shift = held.tile([P, C_BLOCKS], F32, name="shift")
-        nc.vector.tensor_tensor(shift[:], w_mix_col, b_proj_col, MULT)
-        nc.vector.tensor_tensor(shift[:], shift[:], b_mix_col, ADD)
+        nc.vector.tensor_tensor(shift[:], w_mix_col[:], b_proj_col[:], MULT)
+        nc.vector.tensor_tensor(shift[:], shift[:], b_mix_col[:], ADD)
 
         for b in range(C_BLOCKS):
             channels = slice(b * P, (b + 1) * P)

@@ -43,9 +43,9 @@ def tile_mixedrepeatheads_kernel(
             nc.scalar.dma_start(column[:], vector.rearrange("(b p) o -> p (b o)", p=P))
 
         weights = held.tile([P, D_BLOCKS, C], BF16, name="weights")
-        nc.sync.dma_start(weights[:], w_proj.rearrange("(k p) c -> p k c", p=P))
+        nc.sync.dma_start(weights[:], w_proj.rearrange("(p k) c -> p k c", k=D_BLOCKS))
         features = held.tile([P, D_BLOCKS, N], BF16, name="features")
-        nc.sync.dma_start(features[:], x.rearrange("(k p) n -> p k n", p=P))
+        nc.sync.dma_start(features[:], x.rearrange("(p k) n -> p k n", k=D_BLOCKS))
         cached, windows = [], []
         for b in range(C_BLOCKS):
             channels = slice(b * P, (b + 1) * P)

@@ -40,32 +40,34 @@ def tile_mixedrepeatheads_kernel(
             (b_mix_col, b_mix),
             (decay_col, decay),
         ):
-            nc.scalar.dma_start(column[:], vector.rearrange("(b p) o -> p (b o)", p=P))
+            nc.scalar.dma_start(column[:], vector.rearrange("(p b) o -> p (b o)", b=C_BLOCKS))
 
         weights = held.tile([P, D_BLOCKS, C], BF16, name="weights")
         nc.sync.dma_start(weights[:], w_proj.rearrange("(p k) c -> p k c", k=D_BLOCKS))
         features = held.tile([P, D_BLOCKS, N], BF16, name="features")
         nc.sync.dma_start(features[:], x.rearrange("(p k) n -> p k n", k=D_BLOCKS))
+        cache_blocks = cache.rearrange("(p b) n -> p b n", b=C_BLOCKS)
+        base_blocks = base.rearrange("(p b) s -> p b s", b=C_BLOCKS)
+        out_blocks = out.rearrange("(p b) s -> p b s", b=C_BLOCKS)
         cached, windows = [], []
         for b in range(C_BLOCKS):
-            channels = slice(b * P, (b + 1) * P)
             cached.append(held.tile([P, N], F32, name=f"cached{b}"))
-            nc.sync.dma_start(cached[b][:], cache[channels, :])
+            nc.sync.dma_start(cached[b][:], cache_blocks[:, b, :])
             windows.append(held.tile([P, S], F32, name=f"window{b}"))
-            nc.sync.dma_start(windows[b][:], base[channels, :])
+            nc.sync.dma_start(windows[b][:], base_blocks[:, b, :])
 
         coef = held.tile([P, C_BLOCKS], F32, name="coef")
         nc.vector.tensor_scalar(coef[:], decay_col[:], LO, HI, MAX, MIN)
-        column_heads = slice(0, HALF // P)
+        column_heads = slice(0, HALF // C_BLOCKS)
         nc.vector.tensor_tensor(
-            coef[:, column_heads], coef[:, column_heads], w_mix_col[:, column_heads], MULT
+            coef[column_heads, :], coef[column_heads, :], w_mix_col[column_heads, :], MULT
         )
         shift = held.tile([P, C_BLOCKS], F32, name="shift")
         nc.vector.tensor_tensor(shift[:], w_mix_col[:], b_proj_col[:], MULT)
         nc.vector.tensor_tensor(shift[:], shift[:], b_mix_col[:], ADD)
 
         for b in range(C_BLOCKS):
-            channels = slice(b * P, (b + 1) * P)
+            channels = slice(b, C, C_BLOCKS)
             mixed = held.tile([P, N], F32, name=f"mixed{b}")
             for h in range(N_BANKS):
                 entries = slice(h * BANK, (h + 1) * BANK)
@@ -89,4 +91,4 @@ def tile_mixedrepeatheads_kernel(
             nc.scalar.activation(decayed[:], cached[b][:], IDENTITY, scale=coef[:, b : b + 1])
 
             nc.vector.tensor_tensor(windows[b][:].indirect(offsets[:]), mixed[:], decayed[:], ADD)
-            nc.sync.dma_start(out[channels, :], windows[b][:])
+            nc.sync.dma_start(out_blocks[:, b, :], windows[b][:])

@@ -6,6 +6,7 @@ HALF = 128
 LO, HI = 0.9, 1.0
 BANK = 512
 C_BLOCKS, D_BLOCKS, N_BANKS = C // P, D // P, N // BANK
+SQUARE = 32
 
 FLOPS = 2 * C * D * N
 
@@ -30,25 +31,25 @@ def tile_mixedrepeatheads_kernel(
         offsets = held.tile([P, N // 16], U16, name="offsets")
         nc.sync.dma_start(offsets[:], offs)
 
-        b_proj_col, w_mix_col, b_mix_col, decay_col = (
-            held.tile([P, C_BLOCKS], F32, name=name)
-            for name in ("b_proj_col", "w_mix_col", "b_mix_col", "decay_col")
-        )
-        for column, vector in (
-            (w_mix_col, w_mix),
-            (b_proj_col, b_proj),
-            (b_mix_col, b_mix),
-            (decay_col, decay),
-        ):
-            nc.scalar.dma_start(column[:], vector.rearrange("(p b) o -> p (b o)", b=C_BLOCKS))
+        rows = held.tile([P, C_BLOCKS, SQUARE], F32, name="rows", align_bytes=64)
+        nc.vector.memset(rows[:], 0.0)
+        for v, vector in enumerate((w_mix, b_proj, b_mix, decay)):
+            nc.scalar.dma_start(
+                rows[v:P:SQUARE, :, :],
+                vector.rearrange("(b q i) o -> q b (i o)", b=C_BLOCKS, i=SQUARE),
+            )
+        columns = held.tile([P, C_BLOCKS, SQUARE], F32, name="columns", align_bytes=64)
+        for b in range(C_BLOCKS):
+            nc.vector.transpose(columns[:, b, :], rows[:, b, :])
+        w_mix_col, b_proj_col, b_mix_col, decay_col = (columns[:, :, v] for v in range(4))
 
         weights = held.tile([P, D_BLOCKS, C], BF16, name="weights")
         nc.sync.dma_start(weights[:], w_proj.rearrange("(p k) c -> p k c", k=D_BLOCKS))
         features = held.tile([P, D_BLOCKS, N], BF16, name="features")
         nc.sync.dma_start(features[:], x.rearrange("(p k) n -> p k n", k=D_BLOCKS))
-        cache_blocks = cache.rearrange("(p b) n -> p b n", b=C_BLOCKS)
-        base_blocks = base.rearrange("(p b) s -> p b s", b=C_BLOCKS)
-        out_blocks = out.rearrange("(p b) s -> p b s", b=C_BLOCKS)
+        cache_blocks = cache.rearrange("(b p) n -> p b n", b=C_BLOCKS)
+        base_blocks = base.rearrange("(b p) s -> p b s", b=C_BLOCKS)
+        out_blocks = out.rearrange("(b p) s -> p b s", b=C_BLOCKS)
         cached, windows = [], []
         for b in range(C_BLOCKS):
             cached.append(held.tile([P, N], F32, name=f"cached{b}"))
@@ -57,17 +58,17 @@ def tile_mixedrepeatheads_kernel(
             nc.sync.dma_start(windows[b][:], base_blocks[:, b, :])
 
         coef = held.tile([P, C_BLOCKS], F32, name="coef")
-        nc.vector.tensor_scalar(coef[:], decay_col[:], LO, HI, MAX, MIN)
-        column_heads = slice(0, HALF // C_BLOCKS)
+        nc.vector.tensor_scalar(coef[:], decay_col, LO, HI, MAX, MIN)
+        column_heads = slice(0, HALF // P)
         nc.vector.tensor_tensor(
-            coef[column_heads, :], coef[column_heads, :], w_mix_col[column_heads, :], MULT
+            coef[:, column_heads], coef[:, column_heads], w_mix_col[:, column_heads], MULT
         )
         shift = held.tile([P, C_BLOCKS], F32, name="shift")
-        nc.vector.tensor_tensor(shift[:], w_mix_col[:], b_proj_col[:], MULT)
-        nc.vector.tensor_tensor(shift[:], shift[:], b_mix_col[:], ADD)
+        nc.vector.tensor_tensor(shift[:], w_mix_col, b_proj_col, MULT)
+        nc.vector.tensor_tensor(shift[:], shift[:], b_mix_col, ADD)
 
         for b in range(C_BLOCKS):
-            channels = slice(b, C, C_BLOCKS)
+            channels = slice(b * P, (b + 1) * P)
             mixed = held.tile([P, N], F32, name=f"mixed{b}")
             for h in range(N_BANKS):
                 entries = slice(h * BANK, (h + 1) * BANK)

@@ -33,8 +33,13 @@ def tile_mixedrepeatheads_kernel(
 
         rows = held.tile([P, C_BLOCKS, SQUARE], F32, name="rows", align_bytes=64)
         nc.vector.memset(rows[:], 0.0)
+
+        weights = held.tile([P, D_BLOCKS, C], BF16, name="weights")
+        nc.sync.dma_start(weights[:], w_proj.rearrange("(p k) c -> p k c", k=D_BLOCKS))
+        features = held.tile([P, D_BLOCKS, N], BF16, name="features")
+        nc.sync.dma_start(features[:], x.rearrange("(p k) n -> p k n", k=D_BLOCKS))
         for v, vector in enumerate((w_mix, b_proj, b_mix, decay)):
-            nc.scalar.dma_start(
+            nc.sync.dma_start(
                 rows[v:P:SQUARE, :, :],
                 vector.rearrange("(b q i) o -> q b (i o)", b=C_BLOCKS, i=SQUARE),
             )
@@ -42,11 +47,6 @@ def tile_mixedrepeatheads_kernel(
         for b in range(C_BLOCKS):
             nc.vector.transpose(columns[:, b, :], rows[:, b, :])
         w_mix_col, b_proj_col, b_mix_col, decay_col = (columns[:, :, v] for v in range(4))
-
-        weights = held.tile([P, D_BLOCKS, C], BF16, name="weights")
-        nc.sync.dma_start(weights[:], w_proj.rearrange("(p k) c -> p k c", k=D_BLOCKS))
-        features = held.tile([P, D_BLOCKS, N], BF16, name="features")
-        nc.sync.dma_start(features[:], x.rearrange("(p k) n -> p k n", k=D_BLOCKS))
         cache_blocks = cache.rearrange("(b p) n -> p b n", b=C_BLOCKS)
         base_blocks = base.rearrange("(b p) s -> p b s", b=C_BLOCKS)
         out_blocks = out.rearrange("(b p) s -> p b s", b=C_BLOCKS)
@@ -89,7 +89,10 @@ def tile_mixedrepeatheads_kernel(
                     scale=w_mix_col[:, b : b + 1],
                 )
             decayed = held.tile([P, N], F32, name=f"decayed{b}")
-            nc.scalar.activation(decayed[:], cached[b][:], IDENTITY, scale=coef[:, b : b + 1])
+            if b == 0:
+                nc.vector.tensor_scalar_mul(decayed[:], cached[b][:], coef[:, b : b + 1])
+            else:
+                nc.scalar.activation(decayed[:], cached[b][:], IDENTITY, scale=coef[:, b : b + 1])
 
             nc.vector.tensor_tensor(windows[b][:].indirect(offsets[:]), mixed[:], decayed[:], ADD)
             nc.sync.dma_start(out_blocks[:, b, :], windows[b][:])

@@ -34,8 +34,9 @@ def tile_mixedrepeatheads_kernel(
         rows = held.tile([P, C_BLOCKS, SQUARE], F32, name="rows", align_bytes=64)
         nc.vector.memset(rows[:], 0.0)
 
-        weights = held.tile([P, D_BLOCKS, C], BF16, name="weights")
-        nc.sync.dma_start(weights[:], w_proj.rearrange("(p k) c -> p k c", k=D_BLOCKS))
+        w_proj_rows = w_proj.rearrange("(p k) c -> p k c", k=D_BLOCKS)
+        weights = [held.tile([P, D_BLOCKS, P], BF16, name=f"weights{b}") for b in range(C_BLOCKS)]
+        nc.sync.dma_start(weights[0][:], w_proj_rows[:, :, 0:P])
         features = held.tile([P, D_BLOCKS, N], BF16, name="features")
         nc.sync.dma_start(features[:], x.rearrange("(p k) n -> p k n", k=D_BLOCKS))
         for v, vector in enumerate((w_mix, b_proj, b_mix, decay)):
@@ -52,6 +53,8 @@ def tile_mixedrepeatheads_kernel(
         out_blocks = out.rearrange("(b p) s -> p b s", b=C_BLOCKS)
         cached, windows = [], []
         for b in range(C_BLOCKS):
+            if b > 0:
+                nc.sync.dma_start(weights[b][:], w_proj_rows[:, :, b * P : (b + 1) * P])
             cached.append(held.tile([P, N], F32, name=f"cached{b}"))
             nc.sync.dma_start(cached[b][:], cache_blocks[:, b, :])
             windows.append(held.tile([P, S], F32, name=f"window{b}"))
@@ -68,7 +71,6 @@ def tile_mixedrepeatheads_kernel(
         nc.vector.tensor_tensor(shift[:], shift[:], b_mix_col, ADD)
 
         for b in range(C_BLOCKS):
-            channels = slice(b * P, (b + 1) * P)
             mixed = held.tile([P, N], F32, name=f"mixed{b}")
             for h in range(N_BANKS):
                 entries = slice(h * BANK, (h + 1) * BANK)
@@ -76,7 +78,7 @@ def tile_mixedrepeatheads_kernel(
                 for k in range(D_BLOCKS):
                     nc.tensor.matmul(
                         proj[:],
-                        weights[:, k, channels],
+                        weights[b][:, k, :],
                         features[:, k, entries],
                         start=(k == 0),
                         stop=(k == D_BLOCKS - 1),

import concourse.mybir as mybir

P = 128
C, D, S, N = 256, 256, 4096, 1024
HALF = 128
LO, HI = 0.9, 1.0
BANK = 512
C_BLOCKS, D_BLOCKS, N_BANKS = C // P, D // P, N // BANK
SQUARE = 32

FLOPS = 2 * C * D * N

F32, BF16, U16 = mybir.dt.float32, mybir.dt.bfloat16, mybir.dt.uint16
ADD, MULT, MAX, MIN = (
    mybir.AluOpType.add,
    mybir.AluOpType.mult,
    mybir.AluOpType.max,
    mybir.AluOpType.min,
)
IDENTITY = mybir.ActivationFunctionType.Identity


def tile_mixedrepeatheads_kernel(
    tc, base, x, w_proj, b_proj, w_mix, b_mix, decay, cache, offs, out
):
    nc = tc.nc
    with (
        tc.tile_pool(name="held", bufs=1) as held,
        tc.psum_pool(name="psum", bufs=1) as psum,
    ):
        offsets = held.tile([P, N // 16], U16, name="offsets")
        nc.sync.dma_start(offsets[:], offs)

        rows = held.tile([P, C_BLOCKS, SQUARE], F32, name="rows", align_bytes=64)
        nc.vector.memset(rows[:], 0.0)

        w_proj_rows = w_proj.rearrange("(p k) c -> p k c", k=D_BLOCKS)
        weights = [held.tile([P, D_BLOCKS, P], BF16, name=f"weights{b}") for b in range(C_BLOCKS)]
        nc.sync.dma_start(weights[0][:], w_proj_rows[:, :, 0:P])
        features = held.tile([P, D_BLOCKS, N], BF16, name="features")
        nc.sync.dma_start(features[:], x.rearrange("(p k) n -> p k n", k=D_BLOCKS))
        for v, vector in enumerate((w_mix, b_proj, b_mix, decay)):
            nc.sync.dma_start(
                rows[v:P:SQUARE, :, :],
                vector.rearrange("(b q i) o -> q b (i o)", b=C_BLOCKS, i=SQUARE),
            )
        columns = held.tile([P, C_BLOCKS, SQUARE], F32, name="columns", align_bytes=64)
        for b in range(C_BLOCKS):
            nc.vector.transpose(columns[:, b, :], rows[:, b, :])
        w_mix_col, b_proj_col, b_mix_col, decay_col = (columns[:, :, v] for v in range(4))
        cache_blocks = cache.rearrange("(b p) n -> p b n", b=C_BLOCKS)
        base_blocks = base.rearrange("(b p) s -> p b s", b=C_BLOCKS)
        out_blocks = out.rearrange("(b p) s -> p b s", b=C_BLOCKS)
        cached, windows = [], []
        for b in range(C_BLOCKS):
            if b > 0:
                nc.sync.dma_start(weights[b][:], w_proj_rows[:, :, b * P : (b + 1) * P])
            cached.append(held.tile([P, N], F32, name=f"cached{b}"))
            nc.sync.dma_start(cached[b][:], cache_blocks[:, b, :])
            windows.append(held.tile([P, S], F32, name=f"window{b}"))
            nc.sync.dma_start(windows[b][:], base_blocks[:, b, :])

        coef = held.tile([P, C_BLOCKS], F32, name="coef")
        nc.vector.tensor_scalar(coef[:], decay_col, LO, HI, MAX, MIN)
        column_heads = slice(0, HALF // P)
        nc.vector.tensor_tensor(
            coef[:, column_heads], coef[:, column_heads], w_mix_col[:, column_heads], MULT
        )
        shift = held.tile([P, C_BLOCKS], F32, name="shift")
        nc.vector.tensor_tensor(shift[:], w_mix_col, b_proj_col, MULT)
        nc.vector.tensor_tensor(shift[:], shift[:], b_mix_col, ADD)

        for b in range(C_BLOCKS):
            mixed = held.tile([P, N], F32, name=f"mixed{b}")
            for h in range(N_BANKS):
                entries = slice(h * BANK, (h + 1) * BANK)
                proj = psum.tile([P, BANK], F32, name=f"proj{b}_{h}")
                for k in range(D_BLOCKS):
                    nc.tensor.matmul(
                        proj[:],
                        weights[b][:, k, :],
                        features[:, k, entries],
                        start=(k == 0),
                        stop=(k == D_BLOCKS - 1),
                    )
                nc.scalar.activation(
                    mixed[:, entries],
                    proj[:],
                    IDENTITY,
                    bias=shift[:, b : b + 1],
                    scale=w_mix_col[:, b : b + 1],
                )
            decayed = held.tile([P, N], F32, name=f"decayed{b}")
            if b == 0:
                nc.vector.tensor_scalar_mul(decayed[:], cached[b][:], coef[:, b : b + 1])
            else:
                nc.scalar.activation(decayed[:], cached[b][:], IDENTITY, scale=coef[:, b : b + 1])

            nc.vector.tensor_tensor(windows[b][:].indirect(offsets[:]), mixed[:], decayed[:], ADD)
            nc.sync.dma_start(out_blocks[:, b, :], windows[b][:])
